import numpy as np
import ml_dtypes


def mxq(x, axis, fmt="e4m3"):
    dtype, down = {"e4m3": (ml_dtypes.float8_e4m3fn, 7), "e5m2": (ml_dtypes.float8_e5m2, 14)}[fmt]
    v = np.moveaxis(np.asarray(x, np.float32).astype(ml_dtypes.bfloat16).astype(np.float64), axis, -1)
    blocks = v.reshape(v.shape[:-1] + (-1, 32))
    amax = np.abs(blocks).max(-1, keepdims=True)
    byte = np.maximum(np.where(amax > 0, np.frexp(amax)[1] - 1 + 127, 0) - down, 1)
    scale = np.exp2(byte - 127.0)
    codes = (blocks / scale).astype(np.float32).astype(dtype).astype(np.float64)
    return np.moveaxis((codes * scale).reshape(v.shape), -1, axis)


WIDE = False


def mx_kscale(k):
    if not WIDE:
        return np.ones(k)
    levels = np.array([10, -10, 5, -5, 0])
    a = np.random.permutation(np.resize(levels, k // 512 * 4)).reshape(k // 512, 4)
    idx = np.arange(k)
    return np.exp2(a[idx // 512, idx % 128 // 32])


BF16 = ml_dtypes.bfloat16


def bf(x):
    return np.asarray(x, np.float32).astype(BF16)


def f64(x):
    return np.asarray(x).astype(np.float64)


B, S, D, DV, NS, SD = 4, 1024, 1024, 512, 2, 128
R = B * S


def silu(v):
    return v / (1.0 + np.exp(-v))


def setup_inputs():
    s, r, t = mx_kscale(D), mx_kscale(D), mx_kscale(DV)
    return {"x": bf(np.random.standard_normal((B, S, D)) * r),
            "h": bf(np.random.standard_normal((B, S, D)) * s),
            "Wv": bf(np.random.standard_normal((NS, DV, D)) / np.sqrt(D) * t[:, None] / s),
            "W1": bf(np.random.standard_normal((NS, SD, D + DV)) / np.sqrt(D + DV) / np.concatenate([r, t]))}


def reference(x, h, Wv, W1):
    xf = f64(x).reshape(R, D)
    hf = f64(h).reshape(R, D)
    w1 = f64(W1)
    views = mxq(hf, 1, "e4m3") @ mxq(f64(Wv).transpose(0, 2, 1), 1, "e4m3")
    a = mxq(xf, 1, "e4m3") @ mxq(w1[:, :, :D].transpose(0, 2, 1), 1, "e4m3")
    b = mxq(views, 2, "e4m3") @ mxq(w1[:, :, D:].transpose(0, 2, 1), 1, "e4m3")
    return silu(a + b).reshape(NS, B, S, SD)

@@ -1,0 +1,201 @@
+from contextlib import ExitStack
+
+import concourse.masks as masks
+import concourse.mybir as mybir
+
+F32 = mybir.dt.float32
+BF16 = mybir.dt.bfloat16
+U32 = mybir.dt.uint32
+U8 = mybir.dt.uint8
+FP8X4 = mybir.dt.float8_e4m3fn_x4
+SILU = mybir.ActivationFunctionType.Silu
+
+P = 128
+R, D, DV, NS, SD = 4096, 1024, 512, 2, 128
+NSTEP = 16
+FLOPS = 2 * R * NS * (D * DV + D * SD + DV * SD)
+
+
+def tile_distributedb_pa_t_kernel(tc, x, h, Wv, W1, out):
+    nc = tc.nc
+    x_steps = x.rearrange("b (i p j) d -> (b i) p (j d)", p=P, j=2)
+    h_steps = h.rearrange("b (i p j) d -> (b i) p (j d)", p=P, j=2)
+    out_steps = out.rearrange("k b (i p j) f -> (b i) p k (j f)", p=P, j=2)
+    wv_rows = Wv.rearrange("k (u m e) d -> k m u (e d)", u=2, m=P, e=2)
+    w1_rows = W1.rearrange("k s d -> s k d")
+
+    with ExitStack() as ctx:
+        const = ctx.enter_context(tc.tile_pool(name="const", bufs=1))
+        raw = ctx.enter_context(tc.tile_pool(name="raw", bufs=6))
+        grp = ctx.enter_context(tc.tile_pool(name="grp", bufs=3))
+        cod = ctx.enter_context(tc.tile_pool(name="cod", bufs=3))
+        res = ctx.enter_context(tc.tile_pool(name="res", bufs=3))
+        pt = ctx.enter_context(tc.psum_pool(name="pt", bufs=4))
+        pv = ctx.enter_context(tc.psum_pool(name="pv", bufs=3))
+        po = ctx.enter_context(tc.psum_pool(name="po", bufs=1))
+        ctx.enter_context(tc.manual_schedule())
+
+        vcopy = nc.vector.tensor_copy
+        scopy = nc.scalar.copy
+
+        ident = const.tile([P, P], F32, name="ident")
+        masks.make_identity(nc, ident[:])
+        warm = const.tile([P, 8], F32, name="warm")
+        nc.vector.memset(warm[:], 0.0)
+        nc.scalar.activation(out=warm[:], in_=warm[:], func=SILU)
+
+        wv_raw = [const.tile([P, 4096], BF16, name="wv_raw%d" % k) for k in range(NS)]
+        wv_grp = [const.tile([P, 4096], BF16, name="wv_grp%d" % k, align_bytes=64) for k in range(NS)]
+        w1_raw = const.tile([P, 3072], BF16, name="w1_raw")
+        w1_grp = const.tile([P, 3072], BF16, name="w1_grp", align_bytes=64)
+        wv_c = const.tile([P, 2048], U32, name="wv_c", align_bytes=64)
+        wv_s = const.tile([P, 2048], U8, name="wv_s", align_bytes=64)
+        w1_c = const.tile([P, 768], U32, name="w1_c", align_bytes=64)
+        w1_s = const.tile([P, 768], U8, name="w1_s", align_bytes=64)
+
+        h_raw = {}
+        x_raw = {}
+
+        def load_h(i):
+            if i < NSTEP:
+                t = raw.tile([P, 2048], BF16, name="h_raw", tag="h_raw")
+                nc.sync.dma_start(out=t[:], in_=h_steps[i, :, :])
+                h_raw[i] = t
+
+        def load_x(i):
+            if i < NSTEP:
+                t = raw.tile([P, 2048], BF16, name="x_raw", tag="x_raw")
+                nc.sync.dma_start(out=t[:], in_=x_steps[i, :, :])
+                x_raw[i] = t
+
+        def load_wv(k):
+            nc.sync.dma_start(out=wv_raw[k][:].rearrange("p (u c) -> p u c", u=2), in_=wv_rows[k, :, :, :])
+
+        def flip(words, cols, copy, dest):
+            bank = pt.tile([P, 2, 256], F32, name="bank", tag="bank")
+            for u in range(2):
+                for s in range(2):
+                    c0 = cols(u, s)
+                    nc.tensor.transpose(bank[:, u, s * P:(s + 1) * P], words[:, c0:c0 + P], ident[:])
+            copy(out=dest, in_=bank[:].rearrange("p u r -> p r u"))
+
+        def word_view(grouped):
+            return grouped[:].bitcast(F32).rearrange("p (b r u) -> p b r u", r=256, u=2)
+
+        def quantise(grouped, codes, scales, c0, n):
+            nc.vector.quantize_mx(
+                out=codes[:, c0:c0 + n].bitcast(FP8X4),
+                scales=scales[:, c0:c0 + n],
+                in_=grouped,
+            )
+
+        def flip_rows(raw_tile, name, copies):
+            grouped = grp.tile([P, 2048], BF16, name=name, tag=name, align_bytes=64)
+            words = raw_tile[:].bitcast(F32)
+            dest = word_view(grouped)
+            for g in range(2):
+                flip(words, lambda u, s: 512 * s + P * (2 * g + u), copies[g], dest[:, g])
+            return grouped
+
+        def quantise_rows(grouped, name):
+            codes = cod.tile([P, 512], U32, name=name + "_c", tag=name + "_c", align_bytes=64)
+            scales = cod.tile([P, 512], U8, name=name + "_s", tag=name + "_s", align_bytes=64)
+            quantise(grouped[:], codes, scales, 0, 512)
+            return codes, scales
+
+        def prepare_wv(k):
+            words = wv_raw[k][:].bitcast(F32)
+            dest = word_view(wv_grp[k])
+            for g in range(2):
+                for th in range(2):
+                    flip(words, lambda u, s: 512 * (2 * th + s) + P * (2 * g + u),
+                         (vcopy, scopy)[th], dest[:, 2 * g + th])
+            for g in range(2):
+                quantise(wv_grp[k][:, 2048 * g:2048 * (g + 1)], wv_c, wv_s, 1024 * k + 512 * g, 512)
+
+        def prepare_w1():
+            words = w1_raw[:].bitcast(F32)
+            dest = word_view(w1_grp)
+            for g in range(3):
+                flip(words, lambda u, s: 768 * s + P * (2 * g + u), (scopy, vcopy, scopy)[g], dest[:, g])
+            for g in range(3):
+                quantise(w1_grp[:, 1024 * g:1024 * (g + 1)], w1_c, w1_s, 256 * g, 256)
+
+        def mx(acc, a, a_col, b, b_col, start, stop):
+            nc.tensor.matmul_mx(
+                out=acc,
+                lhsT=a[0][:, a_col:a_col + P].bitcast(FP8X4),
+                lhsT_scale=a[1][:, a_col:a_col + P],
+                rhs=b[0][:, b_col:b_col + P].bitcast(FP8X4),
+                rhs_scale=b[1][:, b_col:b_col + P],
+                start=start,
+                stop=stop,
+            )
+
+        wv_q = (wv_c, wv_s)
+        w1_q = (w1_c, w1_s)
+
+        def views(h_q):
+            grouped = grp.tile([P, 2048], BF16, name="v_grp", tag="v_grp", align_bytes=64)
+            dest = grouped[:].rearrange("p (b r t) -> p b r t", r=P, t=4)
+            for k in range(NS):
+                for j in range(2):
+                    acc = pv.tile([P, 4, P], F32, name="v_acc", tag="v_acc")
+                    for t in range(4):
+                        for g in range(2):
+                            mx(acc[:, t, :], wv_q, 1024 * k + 512 * g + P * t, h_q, 256 * g + P * j, g == 0, g == 1)
+                    scopy(out=dest[:, 2 * k + j], in_=acc[:].rearrange("p t r -> p r t"))
+            return grouped
+
+        def finish(i, x_q, v_q):
+            acc = po.tile([P, NS, 2, SD], F32, name="o_acc", tag="o_acc")
+            for j in range(2):
+                for k in range(NS):
+                    for g in range(2):
+                        mx(acc[:, k, j, :], x_q, 256 * g + P * j, w1_q, 256 * g + P * k, g == 0, False)
+                    mx(acc[:, k, j, :], v_q, P * (2 * k + j), w1_q, 512 + P * k, False, True)
+            o_sb = res.tile([P, NS, 2 * SD], F32, name="o_sb", tag="o_sb")
+            nc.scalar.activation(out=o_sb[:], in_=acc[:].rearrange("p k j f -> p k (j f)"), func=SILU)
+            nc.sync.dma_start(out=out_steps[i, :, :, :], in_=o_sb[:])
+
+        load_h(0)
+        load_wv(0)
+        load_wv(1)
+        load_h(1)
+        load_x(0)
+        load_h(2)
+        nc.sync.dma_start(out=w1_raw[:].rearrange("p (k d) -> p k d", k=NS), in_=w1_rows)
+        load_x(1)
+        load_h(3)
+        load_x(2)
+        load_h(4)
+        load_x(3)
+        load_h(5)
+        load_x(4)
+        load_x(5)
+
+        h_q = {}
+        x_q = {}
+        v_q = {}
+        g0 = flip_rows(h_raw[0], "h_grp", (vcopy, scopy))
+        h_q[0] = quantise_rows(g0, "h")
+        prepare_wv(0)
+        prepare_wv(1)
+
+        for i in range(NSTEP + 1):
+            if i < NSTEP:
+                hg = None
+                if i + 1 < NSTEP:
+                    hg = flip_rows(h_raw[i + 1], "h_grp", (vcopy, vcopy))
+                xg = flip_rows(x_raw[i], "x_grp", (vcopy, scopy))
+                if i == 1:
+                    prepare_w1()
+                if hg is not None:
+                    h_q[i + 1] = quantise_rows(hg, "h")
+                x_q[i] = quantise_rows(xg, "x")
+                load_h(i + 6)
+                load_x(i + 6)
+                vg = views(h_q[i])
+                v_q[i] = quantise_rows(vg, "v")
+            if i >= 1:
+                finish(i - 1, x_q[i - 1], v_q[i - 1])

@@ -121,13 +121,13 @@ def tile_distributedb_pa_t_kernel(tc, x, h, Wv, W1, out):
             for g in range(3):
                 quantise(w1_grp[:, 1024 * g:1024 * (g + 1)], w1_c, w1_s, 256 * g, 256)
 
-        def mx(acc, a, a_col, b, b_col, start, stop):
+        def mx(acc, a, a_col, b, b_col, n, start, stop):
             nc.tensor.matmul_mx(
                 out=acc,
                 lhsT=a[0][:, a_col:a_col + P].bitcast(FP8X4),
                 lhsT_scale=a[1][:, a_col:a_col + P],
-                rhs=b[0][:, b_col:b_col + P].bitcast(FP8X4),
-                rhs_scale=b[1][:, b_col:b_col + P],
+                rhs=b[0][:, b_col:b_col + n].bitcast(FP8X4),
+                rhs_scale=b[1][:, b_col:b_col + n],
                 start=start,
                 stop=stop,
             )
@@ -137,14 +137,14 @@ def tile_distributedb_pa_t_kernel(tc, x, h, Wv, W1, out):
 
         def views(h_q):
             grouped = grp.tile([P, 2048], BF16, name="v_grp", tag="v_grp", align_bytes=64)
-            dest = grouped[:].rearrange("p (b r t) -> p b r t", r=P, t=4)
+            dest = grouped[:].rearrange("p (k r t) -> p k r t", k=NS, t=4)
             for k in range(NS):
-                for j in range(2):
-                    acc = pv.tile([P, 4, P], F32, name="v_acc", tag="v_acc")
-                    for t in range(4):
+                for th in range(2):
+                    acc = pv.tile([P, 2, 256], F32, name="v_acc", tag="v_acc")
+                    for t in range(2):
                         for g in range(2):
-                            mx(acc[:, t, :], wv_q, 1024 * k + 512 * g + P * t, h_q, 256 * g + P * j, g == 0, g == 1)
-                    scopy(out=dest[:, 2 * k + j], in_=acc[:].rearrange("p t r -> p r t"))
+                            mx(acc[:, t, :], wv_q, 1024 * k + 512 * g + P * (2 * th + t), h_q, 256 * g, 256, g == 0, g == 1)
+                    scopy(out=dest[:, k, :, 2 * th:2 * th + 2], in_=acc[:].rearrange("p t r -> p r t"))
             return grouped
 
         def finish(i, x_q, v_q):
@@ -152,8 +152,8 @@ def tile_distributedb_pa_t_kernel(tc, x, h, Wv, W1, out):
             for j in range(2):
                 for k in range(NS):
                     for g in range(2):
-                        mx(acc[:, k, j, :], x_q, 256 * g + P * j, w1_q, 256 * g + P * k, g == 0, False)
-                    mx(acc[:, k, j, :], v_q, P * (2 * k + j), w1_q, 512 + P * k, False, True)
+                        mx(acc[:, k, j, :], x_q, 256 * g + P * j, w1_q, 256 * g + P * k, P, g == 0, False)
+                    mx(acc[:, k, j, :], v_q, P * (2 * k + j), w1_q, 512 + P * k, P, False, True)
             o_sb = res.tile([P, NS, 2 * SD], F32, name="o_sb", tag="o_sb")
             nc.scalar.activation(out=o_sb[:], in_=acc[:].rearrange("p k j f -> p k (j f)"), func=SILU)
             nc.sync.dma_start(out=out_steps[i, :, :, :], in_=o_sb[:])
@@ -182,20 +182,24 @@ def tile_distributedb_pa_t_kernel(tc, x, h, Wv, W1, out):
         prepare_wv(0)
         prepare_wv(1)
 
+        v_grp = {}
         for i in range(NSTEP + 1):
+            hg = None
+            xg = None
             if i < NSTEP:
-                hg = None
                 if i + 1 < NSTEP:
                     hg = flip_rows(h_raw[i + 1], "h_grp", (vcopy, vcopy))
-                xg = flip_rows(x_raw[i], "x_grp", (vcopy, scopy))
+                xg = flip_rows(x_raw[i], "x_grp", (vcopy, vcopy))
                 if i == 1:
                     prepare_w1()
-                if hg is not None:
-                    h_q[i + 1] = quantise_rows(hg, "h")
+            if i >= 1:
+                v_q[i - 1] = quantise_rows(v_grp[i - 1], "v")
+            if hg is not None:
+                h_q[i + 1] = quantise_rows(hg, "h")
+            if i < NSTEP:
                 x_q[i] = quantise_rows(xg, "x")
                 load_h(i + 6)
                 load_x(i + 6)
-                vg = views(h_q[i])
-                v_q[i] = quantise_rows(vg, "v")
+                v_grp[i] = views(h_q[i])
             if i >= 1:
                 finish(i - 1, x_q[i - 1], v_q[i - 1])

@@ -13,30 +13,48 @@ SILU = mybir.ActivationFunctionType.Silu
 P = 128
 R, D, DV, NS, SD = 4096, 1024, 512, 2, 128
 NSTEP = 16
+RAW_BUFS = 8
 FLOPS = 2 * R * NS * (D * DV + D * SD + DV * SD)
+
+RUNS = {
+    1: (("x", 0), ("w1", 0), ("h", 2)),
+    2: (("x", 1), ("h", 3), ("x", 2), ("h", 4)),
+    4: (("x", 3), ("h", 5), ("x", 4), ("h", 6), ("x", 5), ("h", 7)),
+    6: (("h", 8), ("h", 9), ("x", 6), ("x", 7)),
+    8: (("h", 10), ("h", 11), ("x", 8), ("x", 9)),
+    10: (("h", 12), ("h", 13), ("x", 10), ("x", 11)),
+    12: (("h", 14), ("h", 15), ("x", 12), ("x", 13)),
+    14: (("x", 14), ("x", 15)),
+}
+FIRST_LOADS = (
+    ("h", 0), ("wv", 0), ("wv", 1), ("wv", 2), ("wv", 3), ("h", 1), ("h", 2), ("x", 0), ("w1", 0),
+    ("h", 3), ("x", 1), ("h", 4), ("x", 2), ("h", 5), ("x", 3), ("h", 6), ("x", 4), ("h", 7), ("x", 5),
+    ("x", 6), ("x", 7),
+)
 
 
 def tile_distributedb_pa_t_kernel(tc, x, h, Wv, W1, out):
     nc = tc.nc
-    x_steps = x.rearrange("b (i p j) d -> (b i) p (j d)", p=P, j=2)
-    h_steps = h.rearrange("b (i p j) d -> (b i) p (j d)", p=P, j=2)
+    rows = {
+        "x": x.rearrange("b (i p j) d -> (b i) p (j d)", p=P, j=2),
+        "h": h.rearrange("b (i p j) d -> (b i) p (j d)", p=P, j=2),
+        "wv": Wv.rearrange("k (u m e) d -> (k u) m (e d)", u=2, m=P, e=2),
+    }
     out_steps = out.rearrange("k b (i p j) f -> (b i) p k (j f)", p=P, j=2)
-    wv_rows = Wv.rearrange("k (u m e) d -> k m u (e d)", u=2, m=P, e=2)
     w1_rows = W1.rearrange("k s d -> s k d")
 
     with ExitStack() as ctx:
         const = ctx.enter_context(tc.tile_pool(name="const", bufs=1))
-        raw = ctx.enter_context(tc.tile_pool(name="raw", bufs=6))
-        grp = ctx.enter_context(tc.tile_pool(name="grp", bufs=3))
-        cod = ctx.enter_context(tc.tile_pool(name="cod", bufs=3))
+        raw_pool = ctx.enter_context(tc.tile_pool(name="raw", bufs=RAW_BUFS))
+        grp = ctx.enter_context(tc.tile_pool(name="grp", bufs=4))
+        cod = ctx.enter_context(tc.tile_pool(name="cod", bufs=4))
         res = ctx.enter_context(tc.tile_pool(name="res", bufs=3))
         pt = ctx.enter_context(tc.psum_pool(name="pt", bufs=4))
         pv = ctx.enter_context(tc.psum_pool(name="pv", bufs=3))
         po = ctx.enter_context(tc.psum_pool(name="po", bufs=1))
         ctx.enter_context(tc.manual_schedule())
 
-        vcopy = nc.vector.tensor_copy
-        scopy = nc.scalar.copy
+        copies = (nc.vector.tensor_copy, nc.scalar.copy)
 
         ident = const.tile([P, P], F32, name="ident")
         masks.make_identity(nc, ident[:])
@@ -44,82 +62,72 @@ def tile_distributedb_pa_t_kernel(tc, x, h, Wv, W1, out):
         nc.vector.memset(warm[:], 0.0)
         nc.scalar.activation(out=warm[:], in_=warm[:], func=SILU)
 
-        wv_raw = [const.tile([P, 4096], BF16, name="wv_raw%d" % k) for k in range(NS)]
-        wv_grp = [const.tile([P, 4096], BF16, name="wv_grp%d" % k, align_bytes=64) for k in range(NS)]
-        w1_raw = const.tile([P, 3072], BF16, name="w1_raw")
-        w1_grp = const.tile([P, 3072], BF16, name="w1_grp", align_bytes=64)
-        wv_c = const.tile([P, 2048], U32, name="wv_c", align_bytes=64)
-        wv_s = const.tile([P, 2048], U8, name="wv_s", align_bytes=64)
-        w1_c = const.tile([P, 768], U32, name="w1_c", align_bytes=64)
-        w1_s = const.tile([P, 768], U8, name="w1_s", align_bytes=64)
+        raw = {}
+        grouped = {}
+        quantised = {}
 
-        h_raw = {}
-        x_raw = {}
+        def load(unit):
+            kind, n = unit
+            if kind == "w1":
+                t = const.tile([P, 3072], BF16, name="w1_raw")
+                nc.sync.dma_start(out=t[:].rearrange("p (k d) -> p k d", k=NS), in_=w1_rows)
+            elif kind == "wv":
+                t = const.tile([P, 2048], BF16, name="wv_raw%d" % n)
+                nc.sync.dma_start(out=t[:], in_=rows[kind][n, :, :])
+            else:
+                t = raw_pool.tile([P, 2048], BF16, name=kind + "_raw", tag=kind + "_raw")
+                nc.sync.dma_start(out=t[:], in_=rows[kind][n, :, :])
+            raw[unit] = t
 
-        def load_h(i):
-            if i < NSTEP:
-                t = raw.tile([P, 2048], BF16, name="h_raw", tag="h_raw")
-                nc.sync.dma_start(out=t[:], in_=h_steps[i, :, :])
-                h_raw[i] = t
-
-        def load_x(i):
-            if i < NSTEP:
-                t = raw.tile([P, 2048], BF16, name="x_raw", tag="x_raw")
-                nc.sync.dma_start(out=t[:], in_=x_steps[i, :, :])
-                x_raw[i] = t
-
-        def load_wv(k):
-            nc.sync.dma_start(out=wv_raw[k][:].rearrange("p (u c) -> p u c", u=2), in_=wv_rows[k, :, :, :])
-
-        def flip(words, cols, copy, dest):
+        def flip(words, pitch, g, copy, dest):
             bank = pt.tile([P, 2, 256], F32, name="bank", tag="bank")
             for u in range(2):
                 for s in range(2):
-                    c0 = cols(u, s)
+                    c0 = pitch * s + P * (2 * g + u)
                     nc.tensor.transpose(bank[:, u, s * P:(s + 1) * P], words[:, c0:c0 + P], ident[:])
             copy(out=dest, in_=bank[:].rearrange("p u r -> p r u"))
 
-        def word_view(grouped):
-            return grouped[:].bitcast(F32).rearrange("p (b r u) -> p b r u", r=256, u=2)
+        def quantise(src, codes, scales):
+            nc.vector.quantize_mx(out=codes.bitcast(FP8X4), scales=scales, in_=src)
 
-        def quantise(grouped, codes, scales, c0, n):
-            nc.vector.quantize_mx(
-                out=codes[:, c0:c0 + n].bitcast(FP8X4),
-                scales=scales[:, c0:c0 + n],
-                in_=grouped,
-            )
-
-        def flip_rows(raw_tile, name, copies):
-            grouped = grp.tile([P, 2048], BF16, name=name, tag=name, align_bytes=64)
-            words = raw_tile[:].bitcast(F32)
-            dest = word_view(grouped)
-            for g in range(2):
-                flip(words, lambda u, s: 512 * s + P * (2 * g + u), copies[g], dest[:, g])
-            return grouped
-
-        def quantise_rows(grouped, name):
-            codes = cod.tile([P, 512], U32, name=name + "_c", tag=name + "_c", align_bytes=64)
-            scales = cod.tile([P, 512], U8, name=name + "_s", tag=name + "_s", align_bytes=64)
-            quantise(grouped[:], codes, scales, 0, 512)
-            return codes, scales
-
-        def prepare_wv(k):
-            words = wv_raw[k][:].bitcast(F32)
-            dest = word_view(wv_grp[k])
-            for g in range(2):
-                for th in range(2):
-                    flip(words, lambda u, s: 512 * (2 * th + s) + P * (2 * g + u),
-                         (vcopy, scopy)[th], dest[:, 2 * g + th])
-            for g in range(2):
-                quantise(wv_grp[k][:, 2048 * g:2048 * (g + 1)], wv_c, wv_s, 1024 * k + 512 * g, 512)
-
-        def prepare_w1():
-            words = w1_raw[:].bitcast(F32)
-            dest = word_view(w1_grp)
-            for g in range(3):
-                flip(words, lambda u, s: 768 * s + P * (2 * g + u), (scopy, vcopy, scopy)[g], dest[:, g])
-            for g in range(3):
-                quantise(w1_grp[:, 1024 * g:1024 * (g + 1)], w1_c, w1_s, 256 * g, 256)
+        def run(units):
+            jobs = []
+            for unit in units:
+                kind, n = unit
+                if kind == "w1":
+                    t = const.tile([P, 3072], BF16, name="w1_grp", align_bytes=64)
+                elif kind == "wv":
+                    t = const.tile([P, 2048], BF16, name="wv_grp%d" % n, align_bytes=64)
+                else:
+                    t = grp.tile([P, 2048], BF16, name=kind + "_grp", tag=kind + "_grp", align_bytes=64)
+                grouped[unit] = t
+                dest = t[:].bitcast(F32).rearrange("p (b r u) -> p b r u", r=256, u=2)
+                words = raw[unit][:].bitcast(F32)
+                for g in range(3 if kind == "w1" else 2):
+                    jobs.append((words, 768 if kind == "w1" else 512, g, dest[:, g]))
+            for n, job in enumerate(jobs):
+                flip(job[0], job[1], job[2], copies[n % 2], job[3])
+            for unit in units:
+                kind, n = unit
+                if kind in ("x", "h") and n + RAW_BUFS < NSTEP:
+                    load((kind, n + RAW_BUFS))
+            for unit in units:
+                kind, n = unit
+                if kind == "w1":
+                    codes = const.tile([P, 768], U32, name="w1_c", align_bytes=64)
+                    scales = const.tile([P, 768], U8, name="w1_s", align_bytes=64)
+                    for g in range(3):
+                        quantise(grouped[unit][:, 1024 * g:1024 * (g + 1)],
+                                 codes[:, 256 * g:256 * (g + 1)], scales[:, 256 * g:256 * (g + 1)])
+                else:
+                    if kind == "wv":
+                        codes = const.tile([P, 512], U32, name="wv_c%d" % n, align_bytes=64)
+                        scales = const.tile([P, 512], U8, name="wv_s%d" % n, align_bytes=64)
+                    else:
+                        codes = cod.tile([P, 512], U32, name=kind + "_c", tag=kind + "_c", align_bytes=64)
+                        scales = cod.tile([P, 512], U8, name=kind + "_s", tag=kind + "_s", align_bytes=64)
+                    quantise(grouped[unit][:], codes[:], scales[:])
+                quantised[unit] = (codes, scales)
 
         def mx(acc, a, a_col, b, b_col, n, start, stop):
             nc.tensor.matmul_mx(
@@ -132,74 +140,59 @@ def tile_distributedb_pa_t_kernel(tc, x, h, Wv, W1, out):
                 stop=stop,
             )
 
-        wv_q = (wv_c, wv_s)
-        w1_q = (w1_c, w1_s)
-
-        def views(h_q):
-            grouped = grp.tile([P, 2048], BF16, name="v_grp", tag="v_grp", align_bytes=64)
-            dest = grouped[:].rearrange("p (k r t) -> p k r t", k=NS, t=4)
-            for k in range(NS):
-                for th in range(2):
-                    acc = pv.tile([P, 2, 256], F32, name="v_acc", tag="v_acc")
-                    for t in range(2):
-                        for g in range(2):
-                            mx(acc[:, t, :], wv_q, 1024 * k + 512 * g + P * (2 * th + t), h_q, 256 * g, 256, g == 0, g == 1)
-                    scopy(out=dest[:, k, :, 2 * th:2 * th + 2], in_=acc[:].rearrange("p t r -> p r t"))
-            return grouped
-
-        def finish(i, x_q, v_q):
-            acc = po.tile([P, NS, 2, SD], F32, name="o_acc", tag="o_acc")
+        def views(i):
+            h_q = quantised[("h", i)]
+            t = grp.tile([P, 2048], BF16, name="v_grp", tag="v_grp", align_bytes=64)
+            codes = cod.tile([P, 512], U32, name="v_c", tag="v_c", align_bytes=64)
+            scales = cod.tile([P, 512], U8, name="v_s", tag="v_s", align_bytes=64)
+            dest = t[:].rearrange("p (b r t) -> p b r t", r=P, t=4)
             for j in range(2):
                 for k in range(NS):
-                    for g in range(2):
-                        mx(acc[:, k, j, :], x_q, 256 * g + P * j, w1_q, 256 * g + P * k, P, g == 0, False)
-                    mx(acc[:, k, j, :], v_q, P * (2 * k + j), w1_q, 512 + P * k, P, False, True)
-            o_sb = res.tile([P, NS, 2 * SD], F32, name="o_sb", tag="o_sb")
-            nc.scalar.activation(out=o_sb[:], in_=acc[:].rearrange("p k j f -> p k (j f)"), func=SILU)
-            nc.sync.dma_start(out=out_steps[i, :, :, :], in_=o_sb[:])
+                    acc = pv.tile([P, 4, P], F32, name="v_acc", tag="v_acc")
+                    for tt in range(4):
+                        for g in range(2):
+                            mx(acc[:, tt, :], quantised[("wv", 2 * k + tt // 2)], 256 * g + P * (tt % 2),
+                               h_q, 256 * g + P * j, P, g == 0, g == 1)
+                    nc.scalar.copy(out=dest[:, 2 * j + k], in_=acc[:].rearrange("p t r -> p r t"))
+                if i == NSTEP - 1:
+                    quantise(t[:, 1024 * j:1024 * (j + 1)], codes[:, 256 * j:256 * (j + 1)], scales[:, 256 * j:256 * (j + 1)])
+            if i < NSTEP - 1:
+                quantise(t[:], codes[:], scales[:])
+            quantised[("v", i)] = (codes, scales)
 
-        load_h(0)
-        load_wv(0)
-        load_wv(1)
-        load_h(1)
-        load_x(0)
-        load_h(2)
-        nc.sync.dma_start(out=w1_raw[:].rearrange("p (k d) -> p k d", k=NS), in_=w1_rows)
-        load_x(1)
-        load_h(3)
-        load_x(2)
-        load_h(4)
-        load_x(3)
-        load_h(5)
-        load_x(4)
-        load_x(5)
+        def products(acc, i, j):
+            x_q = quantised[("x", i)]
+            v_q = quantised[("v", i)]
+            w1_q = quantised[("w1", 0)]
+            for g in range(2):
+                mx(acc.rearrange("p k f -> p (k f)"), x_q, 256 * g + P * j, w1_q, 256 * g, 256, g == 0, False)
+            for k in range(NS):
+                mx(acc[:, k, :], v_q, P * (2 * j + k), w1_q, 512 + P * k, P, False, k == NS - 1)
 
-        h_q = {}
-        x_q = {}
-        v_q = {}
-        g0 = flip_rows(h_raw[0], "h_grp", (vcopy, scopy))
-        h_q[0] = quantise_rows(g0, "h")
-        prepare_wv(0)
-        prepare_wv(1)
+        def finish(i):
+            if i < NSTEP - 1:
+                acc = po.tile([P, 2, NS, SD], F32, name="o_acc", tag="o_acc")
+                for j in range(2):
+                    products(acc[:, j, :, :], i, j)
+                o_sb = res.tile([P, NS, 2, SD], F32, name="o_sb", tag="o_sb")
+                nc.scalar.activation(out=o_sb[:], in_=acc[:].rearrange("p j k f -> p k j f"), func=SILU)
+                nc.sync.dma_start(out=out_steps[i, :, :, :], in_=o_sb[:].rearrange("p k j f -> p k (j f)"))
+            else:
+                for j in range(2):
+                    acc = pv.tile([P, 4, P], F32, name="v_acc", tag="v_acc")
+                    products(acc[:, 0:NS, :], i, j)
+                    o_half = res.tile([P, NS, SD], F32, name="o_half", tag="o_half")
+                    nc.scalar.activation(out=o_half[:], in_=acc[:, 0:NS, :], func=SILU)
+                    nc.sync.dma_start(out=out_steps[i, :, :, SD * j:SD * (j + 1)], in_=o_half[:])
 
-        v_grp = {}
+        for unit in FIRST_LOADS:
+            load(unit)
+        for unit in (("h", 0), ("wv", 0), ("wv", 1), ("wv", 2), ("wv", 3), ("h", 1)):
+            run((unit,))
         for i in range(NSTEP + 1):
-            hg = None
-            xg = None
+            if i in RUNS:
+                run(RUNS[i])
             if i < NSTEP:
-                if i + 1 < NSTEP:
-                    hg = flip_rows(h_raw[i + 1], "h_grp", (vcopy, vcopy))
-                xg = flip_rows(x_raw[i], "x_grp", (vcopy, vcopy))
-                if i == 1:
-                    prepare_w1()
+                views(i)
             if i >= 1:
-                v_q[i - 1] = quantise_rows(v_grp[i - 1], "v")
-            if hg is not None:
-                h_q[i + 1] = quantise_rows(hg, "h")
-            if i < NSTEP:
-                x_q[i] = quantise_rows(xg, "x")
-                load_h(i + 6)
-                load_x(i + 6)
-                v_grp[i] = views(h_q[i])
-            if i >= 1:
-                finish(i - 1, x_q[i - 1], v_q[i - 1])
+                finish(i - 1)

@@ -13,24 +13,20 @@ SILU = mybir.ActivationFunctionType.Silu
 P = 128
 R, D, DV, NS, SD = 4096, 1024, 512, 2, 128
 NSTEP = 16
+LAG = 2
 RAW_BUFS = 8
 FLOPS = 2 * R * NS * (D * DV + D * SD + DV * SD)
 
-RUNS = {
-    1: (("x", 0), ("w1", 0), ("h", 2)),
-    2: (("x", 1), ("h", 3), ("x", 2), ("h", 4)),
-    4: (("x", 3), ("h", 5), ("x", 4), ("h", 6), ("x", 5), ("h", 7)),
-    6: (("h", 8), ("h", 9), ("x", 6), ("x", 7)),
-    8: (("h", 10), ("h", 11), ("x", 8), ("x", 9)),
-    10: (("h", 12), ("h", 13), ("x", 10), ("x", 11)),
-    12: (("h", 14), ("h", 15), ("x", 12), ("x", 13)),
-    14: (("x", 14), ("x", 15)),
-}
-FIRST_LOADS = (
-    ("h", 0), ("wv", 0), ("wv", 1), ("wv", 2), ("wv", 3), ("h", 1), ("h", 2), ("x", 0), ("w1", 0),
-    ("h", 3), ("x", 1), ("h", 4), ("x", 2), ("h", 5), ("x", 3), ("h", 6), ("x", 4), ("h", 7), ("x", 5),
-    ("x", 6), ("x", 7),
-)
+START = (("h", 0), ("wv", 0), ("wv", 1), ("wv", 2), ("wv", 3), ("h", 1))
+
+
+def run_units(i):
+    units = [("h", n) for n in (i + 1, i + 2) if n < NSTEP]
+    units.append(("x", i - 1))
+    if i == 1:
+        units.append(("w1", 0))
+    units.append(("x", i))
+    return units
 
 
 def tile_distributedb_pa_t_kernel(tc, x, h, Wv, W1, out):
@@ -47,11 +43,9 @@ def tile_distributedb_pa_t_kernel(tc, x, h, Wv, W1, out):
         const = ctx.enter_context(tc.tile_pool(name="const", bufs=1))
         raw_pool = ctx.enter_context(tc.tile_pool(name="raw", bufs=RAW_BUFS))
         grp = ctx.enter_context(tc.tile_pool(name="grp", bufs=4))
-        cod = ctx.enter_context(tc.tile_pool(name="cod", bufs=4))
+        cod = ctx.enter_context(tc.tile_pool(name="cod", bufs=5))
         res = ctx.enter_context(tc.tile_pool(name="res", bufs=3))
-        pt = ctx.enter_context(tc.psum_pool(name="pt", bufs=4))
-        pv = ctx.enter_context(tc.psum_pool(name="pv", bufs=3))
-        po = ctx.enter_context(tc.psum_pool(name="po", bufs=1))
+        psum = ctx.enter_context(tc.psum_pool(name="psum", bufs=8))
         ctx.enter_context(tc.manual_schedule())
 
         copies = (nc.vector.tensor_copy, nc.scalar.copy)
@@ -80,7 +74,7 @@ def tile_distributedb_pa_t_kernel(tc, x, h, Wv, W1, out):
             raw[unit] = t
 
         def flip(words, pitch, g, copy, dest):
-            bank = pt.tile([P, 2, 256], F32, name="bank", tag="bank")
+            bank = psum.tile([P, 2, 256], F32, name="bank", tag="bank")
             for u in range(2):
                 for s in range(2):
                     c0 = pitch * s + P * (2 * g + u)
@@ -146,16 +140,17 @@ def tile_distributedb_pa_t_kernel(tc, x, h, Wv, W1, out):
             codes = cod.tile([P, 512], U32, name="v_c", tag="v_c", align_bytes=64)
             scales = cod.tile([P, 512], U8, name="v_s", tag="v_s", align_bytes=64)
             dest = t[:].rearrange("p (b r t) -> p b r t", r=P, t=4)
-            for j in range(2):
-                for k in range(NS):
-                    acc = pv.tile([P, 4, P], F32, name="v_acc", tag="v_acc")
+            for k in range(NS):
+                for j in range(2):
+                    b = 2 * k + j
+                    acc = psum.tile([P, 4, P], F32, name="v_acc", tag="bank")
                     for tt in range(4):
                         for g in range(2):
                             mx(acc[:, tt, :], quantised[("wv", 2 * k + tt // 2)], 256 * g + P * (tt % 2),
                                h_q, 256 * g + P * j, P, g == 0, g == 1)
-                    nc.scalar.copy(out=dest[:, 2 * j + k], in_=acc[:].rearrange("p t r -> p r t"))
-                if i == NSTEP - 1:
-                    quantise(t[:, 1024 * j:1024 * (j + 1)], codes[:, 256 * j:256 * (j + 1)], scales[:, 256 * j:256 * (j + 1)])
+                    nc.scalar.copy(out=dest[:, b], in_=acc[:].rearrange("p t r -> p r t"))
+                    if i == NSTEP - 1:
+                        quantise(t[:, 512 * b:512 * (b + 1)], codes[:, P * b:P * (b + 1)], scales[:, P * b:P * (b + 1)])
             if i < NSTEP - 1:
                 quantise(t[:], codes[:], scales[:])
             quantised[("v", i)] = (codes, scales)
@@ -167,11 +162,11 @@ def tile_distributedb_pa_t_kernel(tc, x, h, Wv, W1, out):
             for g in range(2):
                 mx(acc.rearrange("p k f -> p (k f)"), x_q, 256 * g + P * j, w1_q, 256 * g, 256, g == 0, False)
             for k in range(NS):
-                mx(acc[:, k, :], v_q, P * (2 * j + k), w1_q, 512 + P * k, P, False, k == NS - 1)
+                mx(acc[:, k, :], v_q, P * (2 * k + j), w1_q, 512 + P * k, P, False, k == NS - 1)
 
         def finish(i):
             if i < NSTEP - 1:
-                acc = po.tile([P, 2, NS, SD], F32, name="o_acc", tag="o_acc")
+                acc = psum.tile([P, 2, NS, SD], F32, name="o_acc", tag="bank")
                 for j in range(2):
                     products(acc[:, j, :, :], i, j)
                 o_sb = res.tile([P, NS, 2, SD], F32, name="o_sb", tag="o_sb")
@@ -179,20 +174,25 @@ def tile_distributedb_pa_t_kernel(tc, x, h, Wv, W1, out):
                 nc.sync.dma_start(out=out_steps[i, :, :, :], in_=o_sb[:].rearrange("p k j f -> p k (j f)"))
             else:
                 for j in range(2):
-                    acc = pv.tile([P, 4, P], F32, name="v_acc", tag="v_acc")
-                    products(acc[:, 0:NS, :], i, j)
+                    acc = psum.tile([P, NS, SD], F32, name="o_half_acc", tag="bank")
+                    products(acc[:], i, j)
                     o_half = res.tile([P, NS, SD], F32, name="o_half", tag="o_half")
-                    nc.scalar.activation(out=o_half[:], in_=acc[:, 0:NS, :], func=SILU)
+                    nc.scalar.activation(out=o_half[:], in_=acc[:], func=SILU)
                     nc.sync.dma_start(out=out_steps[i, :, :, SD * j:SD * (j + 1)], in_=o_half[:])
 
-        for unit in FIRST_LOADS:
-            load(unit)
-        for unit in (("h", 0), ("wv", 0), ("wv", 1), ("wv", 2), ("wv", 3), ("h", 1)):
-            run((unit,))
-        for i in range(NSTEP + 1):
-            if i in RUNS:
-                run(RUNS[i])
+        in_order_of_use = list(START)
+        for i in range(1, NSTEP, 2):
+            in_order_of_use.extend(run_units(i))
+        for unit in in_order_of_use:
+            if unit[0] in ("wv", "w1") or unit[1] < RAW_BUFS:
+                load(unit)
+
+        for unit in START:
+            run([unit])
+        for i in range(NSTEP + LAG):
+            if i % 2 == 1 and i < NSTEP:
+                run(run_units(i))
             if i < NSTEP:
                 views(i)
-            if i >= 1:
-                finish(i - 1)
+            if i >= LAG:
+                finish(i - LAG)

@@ -48,7 +48,7 @@ def tile_distributedb_pa_t_kernel(tc, x, h, Wv, W1, out):
         psum = ctx.enter_context(tc.psum_pool(name="psum", bufs=8))
         ctx.enter_context(tc.manual_schedule())
 
-        copies = (nc.vector.tensor_copy, nc.scalar.copy)
+        copies = (nc.vector.tensor_copy, nc.scalar.copy, nc.vector.tensor_copy)
 
         ident = const.tile([P, P], F32, name="ident")
         masks.make_identity(nc, ident[:])
@@ -100,7 +100,7 @@ def tile_distributedb_pa_t_kernel(tc, x, h, Wv, W1, out):
                 for g in range(3 if kind == "w1" else 2):
                     jobs.append((words, 768 if kind == "w1" else 512, g, dest[:, g]))
             for n, job in enumerate(jobs):
-                flip(job[0], job[1], job[2], copies[n % 2], job[3])
+                flip(job[0], job[1], job[2], copies[n % 3], job[3])
             for unit in units:
                 kind, n = unit
                 if kind in ("x", "h") and n + RAW_BUFS < NSTEP:

@@ -48,7 +48,7 @@ def tile_distributedb_pa_t_kernel(tc, x, h, Wv, W1, out):
         psum = ctx.enter_context(tc.psum_pool(name="psum", bufs=8))
         ctx.enter_context(tc.manual_schedule())
 
-        copies = (nc.vector.tensor_copy, nc.scalar.copy, nc.vector.tensor_copy)
+        copies = (nc.vector.tensor_copy, nc.scalar.copy)
 
         ident = const.tile([P, P], F32, name="ident")
         masks.make_identity(nc, ident[:])
@@ -100,7 +100,7 @@ def tile_distributedb_pa_t_kernel(tc, x, h, Wv, W1, out):
                 for g in range(3 if kind == "w1" else 2):
                     jobs.append((words, 768 if kind == "w1" else 512, g, dest[:, g]))
             for n, job in enumerate(jobs):
-                flip(job[0], job[1], job[2], copies[n % 3], job[3])
+                flip(job[0], job[1], job[2], copies[n % 2], job[3])
             for unit in units:
                 kind, n = unit
                 if kind in ("x", "h") and n + RAW_BUFS < NSTEP:
@@ -139,18 +139,21 @@ def tile_distributedb_pa_t_kernel(tc, x, h, Wv, W1, out):
             t = grp.tile([P, 2048], BF16, name="v_grp", tag="v_grp", align_bytes=64)
             codes = cod.tile([P, 512], U32, name="v_c", tag="v_c", align_bytes=64)
             scales = cod.tile([P, 512], U8, name="v_s", tag="v_s", align_bytes=64)
-            dest = t[:].rearrange("p (b r t) -> p b r t", r=P, t=4)
             for k in range(NS):
-                for j in range(2):
-                    b = 2 * k + j
-                    acc = psum.tile([P, 4, P], F32, name="v_acc", tag="bank")
-                    for tt in range(4):
+                flat = grp.tile([P, 4, 256], BF16, name="v_flat", tag="v_flat")
+                for th in range(2):
+                    acc = psum.tile([P, 2, 256], F32, name="v_acc", tag="bank")
+                    for t2 in range(2):
                         for g in range(2):
-                            mx(acc[:, tt, :], quantised[("wv", 2 * k + tt // 2)], 256 * g + P * (tt % 2),
-                               h_q, 256 * g + P * j, P, g == 0, g == 1)
-                    nc.scalar.copy(out=dest[:, b], in_=acc[:].rearrange("p t r -> p r t"))
-                    if i == NSTEP - 1:
-                        quantise(t[:, 512 * b:512 * (b + 1)], codes[:, P * b:P * (b + 1)], scales[:, P * b:P * (b + 1)])
+                            mx(acc[:, t2, :], quantised[("wv", 2 * k + th)], 256 * g + P * t2,
+                               h_q, 256 * g, 256, g == 0, g == 1)
+                    nc.scalar.copy(out=flat[:, 2 * th:2 * th + 2, :], in_=acc[:])
+                nc.vector.tensor_copy(
+                    out=t[:, 1024 * k:1024 * (k + 1)].rearrange("p (c i t) -> p c t i", i=4, t=4),
+                    in_=flat[:].rearrange("p t (c i) -> p c t i", i=4),
+                )
+                if i == NSTEP - 1:
+                    quantise(t[:, 1024 * k:1024 * (k + 1)], codes[:, 256 * k:256 * (k + 1)], scales[:, 256 * k:256 * (k + 1)])
             if i < NSTEP - 1:
                 quantise(t[:], codes[:], scales[:])
             quantised[("v", i)] = (codes, scales)

@@ -11,17 +11,21 @@ FP8X4 = mybir.dt.float8_e4m3fn_x4
 SILU = mybir.ActivationFunctionType.Silu
 
 P = 128
-R, D, DV, NS, SD = 4096, 1024, 512, 2, 128
-NSTEP = 16
+ROWS, D, DV, SUBNETS, SD = 4096, 1024, 512, 2, 128
+FLOPS = 2 * ROWS * SUBNETS * (D * DV + D * SD + DV * SD)
+
+STEP_ROWS = 2 * P
+STEPS = ROWS // STEP_ROWS
 LAG = 2
 RAW_BUFS = 8
-FLOPS = 2 * R * NS * (D * DV + D * SD + DV * SD)
 
-START = (("h", 0), ("wv", 0), ("wv", 1), ("wv", 2), ("wv", 3), ("h", 1))
+PASSES = {"x": D // 512, "h": D // 512, "wv": D // 512, "w1": (D + DV) // 512}
+WEIGHTS = ("wv", "w1")
+FIRST_UNITS = (("h", 0), ("wv", 0), ("wv", 1), ("wv", 2), ("wv", 3), ("h", 1))
 
 
-def run_units(i):
-    units = [("h", n) for n in (i + 1, i + 2) if n < NSTEP]
+def units_before_step(i):
+    units = [("h", n) for n in (i + 1, i + 2) if n < STEPS]
     units.append(("x", i - 1))
     if i == 1:
         units.append(("w1", 0))
@@ -31,171 +35,144 @@ def run_units(i):
 
 def tile_distributedb_pa_t_kernel(tc, x, h, Wv, W1, out):
     nc = tc.nc
-    rows = {
-        "x": x.rearrange("b (i p j) d -> (b i) p (j d)", p=P, j=2),
-        "h": h.rearrange("b (i p j) d -> (b i) p (j d)", p=P, j=2),
-        "wv": Wv.rearrange("k (u m e) d -> (k u) m (e d)", u=2, m=P, e=2),
+    sources = {
+        "x": x.rearrange("b (i p j) d -> (b i) p j d", p=P, j=2),
+        "h": h.rearrange("b (i p j) d -> (b i) p j d", p=P, j=2),
+        "wv": Wv.rearrange("k (u p e) d -> (k u) p e d", u=2, p=P, e=2),
+        "w1": W1.rearrange("(o k) p d -> o p k d", o=1),
     }
     out_steps = out.rearrange("k b (i p j) f -> (b i) p k (j f)", p=P, j=2)
-    w1_rows = W1.rearrange("k s d -> s k d")
 
     with ExitStack() as ctx:
-        const = ctx.enter_context(tc.tile_pool(name="const", bufs=1))
+        keep = ctx.enter_context(tc.tile_pool(name="keep", bufs=1))
         raw_pool = ctx.enter_context(tc.tile_pool(name="raw", bufs=RAW_BUFS))
-        grp = ctx.enter_context(tc.tile_pool(name="grp", bufs=4))
-        cod = ctx.enter_context(tc.tile_pool(name="cod", bufs=5))
-        res = ctx.enter_context(tc.tile_pool(name="res", bufs=3))
+        bf16_pool = ctx.enter_context(tc.tile_pool(name="bf16", bufs=4))
+        mx_pool = ctx.enter_context(tc.tile_pool(name="mx", bufs=5))
+        out_pool = ctx.enter_context(tc.tile_pool(name="outs", bufs=3))
         psum = ctx.enter_context(tc.psum_pool(name="psum", bufs=8))
         ctx.enter_context(tc.manual_schedule())
 
-        copies = (nc.vector.tensor_copy, nc.scalar.copy)
-
-        ident = const.tile([P, P], F32, name="ident")
-        masks.make_identity(nc, ident[:])
-        warm = const.tile([P, 8], F32, name="warm")
-        nc.vector.memset(warm[:], 0.0)
-        nc.scalar.activation(out=warm[:], in_=warm[:], func=SILU)
+        identity = keep.tile([P, P], F32, name="identity")
+        masks.make_identity(nc, identity[:])
+        dummy = keep.tile([P, 8], F32, name="dummy")
+        nc.vector.memset(dummy[:], 0.0)
+        nc.scalar.activation(out=dummy[:], in_=dummy[:], func=SILU)
 
         raw = {}
-        grouped = {}
-        quantised = {}
+        mx_operand = {}
+
+        def new_tile(pool, unit, role, width, dtype):
+            kind, n = unit
+            if kind in WEIGHTS:
+                return keep.tile([P, width], dtype, name="%s%d_%s" % (kind, n, role), align_bytes=64)
+            return pool.tile([P, width], dtype, name=kind + "_" + role, tag=kind + "_" + role, align_bytes=64)
 
         def load(unit):
             kind, n = unit
-            if kind == "w1":
-                t = const.tile([P, 3072], BF16, name="w1_raw")
-                nc.sync.dma_start(out=t[:].rearrange("p (k d) -> p k d", k=NS), in_=w1_rows)
-            elif kind == "wv":
-                t = const.tile([P, 2048], BF16, name="wv_raw%d" % n)
-                nc.sync.dma_start(out=t[:], in_=rows[kind][n, :, :])
-            else:
-                t = raw_pool.tile([P, 2048], BF16, name=kind + "_raw", tag=kind + "_raw")
-                nc.sync.dma_start(out=t[:], in_=rows[kind][n, :, :])
-            raw[unit] = t
+            raw[unit] = new_tile(raw_pool, unit, "raw", 1024 * PASSES[kind], BF16)
+            nc.sync.dma_start(out=raw[unit][:].rearrange("p (s d) -> p s d", s=2), in_=sources[kind][n, :, :, :])
 
-        def flip(words, pitch, g, copy, dest):
-            bank = psum.tile([P, 2, 256], F32, name="bank", tag="bank")
-            for u in range(2):
-                for s in range(2):
-                    c0 = pitch * s + P * (2 * g + u)
-                    nc.tensor.transpose(bank[:, u, s * P:(s + 1) * P], words[:, c0:c0 + P], ident[:])
-            copy(out=dest, in_=bank[:].rearrange("p u r -> p r u"))
+        def quantise(values, unit):
+            width = values.shape[1]
+            codes = new_tile(mx_pool, unit, "codes", width // 4, U32)
+            scales = new_tile(mx_pool, unit, "scales", width // 4, U8)
+            for c in range(0, width, 2048):
+                w = min(2048, width - c)
+                nc.vector.quantize_mx(
+                    out=codes[:, c // 4:(c + w) // 4].bitcast(FP8X4),
+                    scales=scales[:, c // 4:(c + w) // 4],
+                    in_=values[:, c:c + w],
+                )
+            mx_operand[unit] = (codes, scales)
 
-        def quantise(src, codes, scales):
-            nc.vector.quantize_mx(out=codes.bitcast(FP8X4), scales=scales, in_=src)
-
-        def run(units):
-            jobs = []
+        def transpose_run(units):
+            copies = (nc.vector.tensor_copy, nc.scalar.copy)
+            grouped = {}
+            banks = 0
             for unit in units:
-                kind, n = unit
-                if kind == "w1":
-                    t = const.tile([P, 3072], BF16, name="w1_grp", align_bytes=64)
-                elif kind == "wv":
-                    t = const.tile([P, 2048], BF16, name="wv_grp%d" % n, align_bytes=64)
-                else:
-                    t = grp.tile([P, 2048], BF16, name=kind + "_grp", tag=kind + "_grp", align_bytes=64)
-                grouped[unit] = t
-                dest = t[:].bitcast(F32).rearrange("p (b r u) -> p b r u", r=256, u=2)
+                passes = PASSES[unit[0]]
                 words = raw[unit][:].bitcast(F32)
-                for g in range(3 if kind == "w1" else 2):
-                    jobs.append((words, 768 if kind == "w1" else 512, g, dest[:, g]))
-            for n, job in enumerate(jobs):
-                flip(job[0], job[1], job[2], copies[n % 2], job[3])
-            for unit in units:
-                kind, n = unit
-                if kind in ("x", "h") and n + RAW_BUFS < NSTEP:
+                grouped[unit] = new_tile(bf16_pool, unit, "grouped", 1024 * passes, BF16)
+                dest = grouped[unit][:].bitcast(F32).rearrange("p (g r u) -> p g r u", r=2 * P, u=2)
+                for g in range(passes):
+                    bank = psum.tile([P, 2, 2 * P], F32, name="flipped", tag="bank")
+                    for u in range(2):
+                        for s in range(2):
+                            first = 256 * passes * s + 256 * g + P * u
+                            nc.tensor.transpose(bank[:, u, P * s:P * (s + 1)], words[:, first:first + P], identity[:])
+                    copies[banks % 2](out=dest[:, g], in_=bank[:].rearrange("p u r -> p r u"))
+                    banks += 1
+            for kind, n in units:
+                if kind not in WEIGHTS and n + RAW_BUFS < STEPS:
                     load((kind, n + RAW_BUFS))
             for unit in units:
-                kind, n = unit
-                if kind == "w1":
-                    codes = const.tile([P, 768], U32, name="w1_c", align_bytes=64)
-                    scales = const.tile([P, 768], U8, name="w1_s", align_bytes=64)
-                    for g in range(3):
-                        quantise(grouped[unit][:, 1024 * g:1024 * (g + 1)],
-                                 codes[:, 256 * g:256 * (g + 1)], scales[:, 256 * g:256 * (g + 1)])
-                else:
-                    if kind == "wv":
-                        codes = const.tile([P, 512], U32, name="wv_c%d" % n, align_bytes=64)
-                        scales = const.tile([P, 512], U8, name="wv_s%d" % n, align_bytes=64)
-                    else:
-                        codes = cod.tile([P, 512], U32, name=kind + "_c", tag=kind + "_c", align_bytes=64)
-                        scales = cod.tile([P, 512], U8, name=kind + "_s", tag=kind + "_s", align_bytes=64)
-                    quantise(grouped[unit][:], codes[:], scales[:])
-                quantised[unit] = (codes, scales)
+                quantise(grouped[unit][:], unit)
 
-        def mx(acc, a, a_col, b, b_col, n, start, stop):
+        def mx_pass(acc, stationary, s_col, moving, m_col, n, start, stop):
             nc.tensor.matmul_mx(
                 out=acc,
-                lhsT=a[0][:, a_col:a_col + P].bitcast(FP8X4),
-                lhsT_scale=a[1][:, a_col:a_col + P],
-                rhs=b[0][:, b_col:b_col + n].bitcast(FP8X4),
-                rhs_scale=b[1][:, b_col:b_col + n],
+                lhsT=stationary[0][:, s_col:s_col + P].bitcast(FP8X4),
+                lhsT_scale=stationary[1][:, s_col:s_col + P],
+                rhs=moving[0][:, m_col:m_col + n].bitcast(FP8X4),
+                rhs_scale=moving[1][:, m_col:m_col + n],
                 start=start,
                 stop=stop,
             )
 
+        regrouped = {}
+
         def views(i):
-            h_q = quantised[("h", i)]
-            t = grp.tile([P, 2048], BF16, name="v_grp", tag="v_grp", align_bytes=64)
-            codes = cod.tile([P, 512], U32, name="v_c", tag="v_c", align_bytes=64)
-            scales = cod.tile([P, 512], U8, name="v_s", tag="v_s", align_bytes=64)
-            for k in range(NS):
-                flat = grp.tile([P, 4, 256], BF16, name="v_flat", tag="v_flat")
-                for th in range(2):
-                    acc = psum.tile([P, 2, 256], F32, name="v_acc", tag="bank")
-                    for t2 in range(2):
-                        for g in range(2):
-                            mx(acc[:, t2, :], quantised[("wv", 2 * k + th)], 256 * g + P * t2,
-                               h_q, 256 * g, 256, g == 0, g == 1)
-                    nc.scalar.copy(out=flat[:, 2 * th:2 * th + 2, :], in_=acc[:])
+            for k in range(SUBNETS):
+                half = SUBNETS * i + k
+                by_tile = bf16_pool.tile([P, 4, STEP_ROWS], BF16, name="views_by_tile")
+                for u in range(2):
+                    bank = psum.tile([P, 2, STEP_ROWS], F32, name="views_acc", tag="bank")
+                    for e in range(2):
+                        for g in range(PASSES["h"]):
+                            mx_pass(bank[:, e, :], mx_operand[("wv", 2 * k + u)], 256 * g + P * e,
+                                    mx_operand[("h", i)], 256 * g, STEP_ROWS, g == 0, g == PASSES["h"] - 1)
+                    nc.scalar.copy(out=by_tile[:, 2 * u:2 * u + 2, :], in_=bank[:])
+                regrouped[half] = bf16_pool.tile([P, 4 * STEP_ROWS], BF16, name="views_regrouped", align_bytes=64)
                 nc.vector.tensor_copy(
-                    out=t[:, 1024 * k:1024 * (k + 1)].rearrange("p (c i t) -> p c t i", i=4, t=4),
-                    in_=flat[:].rearrange("p t (c i) -> p c t i", i=4),
+                    out=regrouped[half][:].rearrange("p (c r t) -> p c t r", r=4, t=4),
+                    in_=by_tile[:].rearrange("p t (c r) -> p c t r", r=4),
                 )
-                if i == NSTEP - 1:
-                    quantise(t[:, 1024 * k:1024 * (k + 1)], codes[:, 256 * k:256 * (k + 1)], scales[:, 256 * k:256 * (k + 1)])
-            if i < NSTEP - 1:
-                quantise(t[:], codes[:], scales[:])
-            quantised[("v", i)] = (codes, scales)
+                if half > 0:
+                    quantise(regrouped[half - 1][:], ("v", half - 1))
+                if half == SUBNETS * STEPS - 1:
+                    quantise(regrouped[half][:], ("v", half))
 
         def products(acc, i, j):
-            x_q = quantised[("x", i)]
-            v_q = quantised[("v", i)]
-            w1_q = quantised[("w1", 0)]
-            for g in range(2):
-                mx(acc.rearrange("p k f -> p (k f)"), x_q, 256 * g + P * j, w1_q, 256 * g, 256, g == 0, False)
-            for k in range(NS):
-                mx(acc[:, k, :], v_q, P * (2 * k + j), w1_q, 512 + P * k, P, False, k == NS - 1)
+            for g in range(PASSES["x"]):
+                mx_pass(acc.rearrange("p k f -> p (k f)"), mx_operand[("x", i)], 256 * g + P * j,
+                        mx_operand[("w1", 0)], 256 * g, SUBNETS * SD, g == 0, False)
+            for k in range(SUBNETS):
+                mx_pass(acc[:, k, :], mx_operand[("v", SUBNETS * i + k)], P * j,
+                        mx_operand[("w1", 0)], 256 * PASSES["x"] + SD * k, SD, False, k == SUBNETS - 1)
 
         def finish(i):
-            if i < NSTEP - 1:
-                acc = psum.tile([P, 2, NS, SD], F32, name="o_acc", tag="bank")
-                for j in range(2):
-                    products(acc[:, j, :, :], i, j)
-                o_sb = res.tile([P, NS, 2, SD], F32, name="o_sb", tag="o_sb")
-                nc.scalar.activation(out=o_sb[:], in_=acc[:].rearrange("p j k f -> p k j f"), func=SILU)
-                nc.sync.dma_start(out=out_steps[i, :, :, :], in_=o_sb[:].rearrange("p k j f -> p k (j f)"))
-            else:
-                for j in range(2):
-                    acc = psum.tile([P, NS, SD], F32, name="o_half_acc", tag="bank")
-                    products(acc[:], i, j)
-                    o_half = res.tile([P, NS, SD], F32, name="o_half", tag="o_half")
-                    nc.scalar.activation(out=o_half[:], in_=acc[:], func=SILU)
-                    nc.sync.dma_start(out=out_steps[i, :, :, SD * j:SD * (j + 1)], in_=o_half[:])
+            for tiles in (((0,), (1,)) if i == STEPS - 1 else ((0, 1),)):
+                bank = psum.tile([P, len(tiles), SUBNETS, SD], F32, name="out_acc", tag="bank")
+                for n, j in enumerate(tiles):
+                    products(bank[:, n, :, :], i, j)
+                result = out_pool.tile([P, SUBNETS, len(tiles), SD], F32, name="result")
+                nc.scalar.activation(out=result[:], in_=bank[:].rearrange("p j k f -> p k j f"), func=SILU)
+                nc.sync.dma_start(out=out_steps[i, :, :, SD * tiles[0]:SD * (tiles[0] + len(tiles))],
+                                  in_=result[:].rearrange("p k j f -> p k (j f)"))
 
-        in_order_of_use = list(START)
-        for i in range(1, NSTEP, 2):
-            in_order_of_use.extend(run_units(i))
+        in_order_of_use = list(FIRST_UNITS)
+        for i in range(1, STEPS, 2):
+            in_order_of_use.extend(units_before_step(i))
         for unit in in_order_of_use:
-            if unit[0] in ("wv", "w1") or unit[1] < RAW_BUFS:
+            if unit[0] in WEIGHTS or unit[1] < RAW_BUFS:
                 load(unit)
 
-        for unit in START:
-            run([unit])
-        for i in range(NSTEP + LAG):
-            if i % 2 == 1 and i < NSTEP:
-                run(run_units(i))
-            if i < NSTEP:
+        for unit in FIRST_UNITS:
+            transpose_run([unit])
+        for i in range(STEPS + LAG):
+            if i % 2 == 1 and i < STEPS:
+                transpose_run(units_before_step(i))
+            if i < STEPS:
                 views(i)
             if i >= LAG:
                 finish(i - LAG)

@@ -14,12 +14,15 @@ P = 128
 ROWS, D, DV, SUBNETS, SD = 4096, 1024, 512, 2, 128
 FLOPS = 2 * ROWS * SUBNETS * (D * DV + D * SD + DV * SD)
 
-STEP_ROWS = 2 * P
-STEPS = ROWS // STEP_ROWS
+K_PASS = 4 * P
+WORDS = K_PASS // 2
+UNIT_ROWS = 2 * P
+
+STEPS = ROWS // UNIT_ROWS
 LAG = 2
 RAW_BUFS = 8
 
-PASSES = {"x": D // 512, "h": D // 512, "wv": D // 512, "w1": (D + DV) // 512}
+PASSES = {"x": D // K_PASS, "h": D // K_PASS, "wv": D // K_PASS, "w1": (D + DV) // K_PASS}
 WEIGHTS = ("wv", "w1")
 FIRST_UNITS = (("h", 0), ("wv", 0), ("wv", 1), ("wv", 2), ("wv", 3), ("h", 1))
 
@@ -47,8 +50,8 @@ def tile_distributedb_pa_t_kernel(tc, x, h, Wv, W1, out):
         keep = ctx.enter_context(tc.tile_pool(name="keep", bufs=1))
         raw_pool = ctx.enter_context(tc.tile_pool(name="raw", bufs=RAW_BUFS))
         bf16_pool = ctx.enter_context(tc.tile_pool(name="bf16", bufs=4))
-        mx_pool = ctx.enter_context(tc.tile_pool(name="mx", bufs=5))
-        out_pool = ctx.enter_context(tc.tile_pool(name="outs", bufs=3))
+        mx_pool = ctx.enter_context(tc.tile_pool(name="mx", bufs=6))
+        out_pool = ctx.enter_context(tc.tile_pool(name="outs", bufs=5))
         psum = ctx.enter_context(tc.psum_pool(name="psum", bufs=8))
         ctx.enter_context(tc.manual_schedule())
 
@@ -60,6 +63,7 @@ def tile_distributedb_pa_t_kernel(tc, x, h, Wv, W1, out):
 
         raw = {}
         mx_operand = {}
+        regrouped = {}
 
         def new_tile(pool, unit, role, width, dtype):
             kind, n = unit
@@ -69,36 +73,42 @@ def tile_distributedb_pa_t_kernel(tc, x, h, Wv, W1, out):
 
         def load(unit):
             kind, n = unit
-            raw[unit] = new_tile(raw_pool, unit, "raw", 1024 * PASSES[kind], BF16)
+            raw[unit] = new_tile(raw_pool, unit, "raw", 2 * K_PASS * PASSES[kind], BF16)
             nc.sync.dma_start(out=raw[unit][:].rearrange("p (s d) -> p s d", s=2), in_=sources[kind][n, :, :, :])
 
         def quantise(values, unit):
             width = values.shape[1]
             codes = new_tile(mx_pool, unit, "codes", width // 4, U32)
             scales = new_tile(mx_pool, unit, "scales", width // 4, U8)
-            for c in range(0, width, 2048):
-                w = min(2048, width - c)
+            for col in range(0, width, 2048):
+                end = min(col + 2048, width)
                 nc.vector.quantize_mx(
-                    out=codes[:, c // 4:(c + w) // 4].bitcast(FP8X4),
-                    scales=scales[:, c // 4:(c + w) // 4],
-                    in_=values[:, c:c + w],
+                    out=codes[:, col // 4:end // 4].bitcast(FP8X4),
+                    scales=scales[:, col // 4:end // 4],
+                    in_=values[:, col:end],
                 )
             mx_operand[unit] = (codes, scales)
 
+        def quantise_views(before):
+            for half in sorted(regrouped):
+                if half < before and ("v", half) not in mx_operand:
+                    quantise(regrouped[half][:], ("v", half))
+
         def transpose_run(units):
+            quantise_views(before=len(regrouped))
             copies = (nc.vector.tensor_copy, nc.scalar.copy)
             grouped = {}
             banks = 0
             for unit in units:
                 passes = PASSES[unit[0]]
                 words = raw[unit][:].bitcast(F32)
-                grouped[unit] = new_tile(bf16_pool, unit, "grouped", 1024 * passes, BF16)
-                dest = grouped[unit][:].bitcast(F32).rearrange("p (g r u) -> p g r u", r=2 * P, u=2)
+                grouped[unit] = new_tile(bf16_pool, unit, "grouped", 2 * K_PASS * passes, BF16)
+                dest = grouped[unit][:].bitcast(F32).rearrange("p (g r u) -> p g r u", r=UNIT_ROWS, u=2)
                 for g in range(passes):
-                    bank = psum.tile([P, 2, 2 * P], F32, name="flipped", tag="bank")
+                    bank = psum.tile([P, 2, UNIT_ROWS], F32, name="flipped", tag="bank")
                     for u in range(2):
                         for s in range(2):
-                            first = 256 * passes * s + 256 * g + P * u
+                            first = WORDS * (passes * s + g) + P * u
                             nc.tensor.transpose(bank[:, u, P * s:P * (s + 1)], words[:, first:first + P], identity[:])
                     copies[banks % 2](out=dest[:, g], in_=bank[:].rearrange("p u r -> p r u"))
                     banks += 1
@@ -108,56 +118,51 @@ def tile_distributedb_pa_t_kernel(tc, x, h, Wv, W1, out):
             for unit in units:
                 quantise(grouped[unit][:], unit)
 
-        def mx_pass(acc, stationary, s_col, moving, m_col, n, start, stop):
+        def mx_pass(acc, stationary, s_col, moving, m_col, m_cols, start, stop):
             nc.tensor.matmul_mx(
                 out=acc,
                 lhsT=stationary[0][:, s_col:s_col + P].bitcast(FP8X4),
                 lhsT_scale=stationary[1][:, s_col:s_col + P],
-                rhs=moving[0][:, m_col:m_col + n].bitcast(FP8X4),
-                rhs_scale=moving[1][:, m_col:m_col + n],
+                rhs=moving[0][:, m_col:m_col + m_cols].bitcast(FP8X4),
+                rhs_scale=moving[1][:, m_col:m_col + m_cols],
                 start=start,
                 stop=stop,
             )
 
-        regrouped = {}
-
         def views(i):
             for k in range(SUBNETS):
                 half = SUBNETS * i + k
-                by_tile = bf16_pool.tile([P, 4, STEP_ROWS], BF16, name="views_by_tile")
+                by_tile = bf16_pool.tile([P, 4, UNIT_ROWS], BF16, name="views_by_tile")
                 for u in range(2):
-                    bank = psum.tile([P, 2, STEP_ROWS], F32, name="views_acc", tag="bank")
+                    bank = psum.tile([P, 2, UNIT_ROWS], F32, name="views_acc", tag="bank")
                     for e in range(2):
                         for g in range(PASSES["h"]):
-                            mx_pass(bank[:, e, :], mx_operand[("wv", 2 * k + u)], 256 * g + P * e,
-                                    mx_operand[("h", i)], 256 * g, STEP_ROWS, g == 0, g == PASSES["h"] - 1)
+                            mx_pass(bank[:, e, :], mx_operand[("wv", 2 * k + u)], UNIT_ROWS * g + P * e,
+                                    mx_operand[("h", i)], UNIT_ROWS * g, UNIT_ROWS, g == 0, g == PASSES["h"] - 1)
                     nc.scalar.copy(out=by_tile[:, 2 * u:2 * u + 2, :], in_=bank[:])
-                regrouped[half] = bf16_pool.tile([P, 4 * STEP_ROWS], BF16, name="views_regrouped", align_bytes=64)
+                regrouped[half] = bf16_pool.tile([P, 4 * UNIT_ROWS], BF16, name="views_regrouped", align_bytes=64)
                 nc.vector.tensor_copy(
-                    out=regrouped[half][:].rearrange("p (c r t) -> p c t r", r=4, t=4),
-                    in_=by_tile[:].rearrange("p t (c r) -> p c t r", r=4),
+                    out=regrouped[half][:].rearrange("p (a r t) -> p a t r", r=4, t=4),
+                    in_=by_tile[:].rearrange("p t (a r) -> p a t r", r=4),
                 )
-                if half > 0:
-                    quantise(regrouped[half - 1][:], ("v", half - 1))
-                if half == SUBNETS * STEPS - 1:
-                    quantise(regrouped[half][:], ("v", half))
+                quantise_views(before=half + 1 if i == STEPS - 1 else half)
 
         def products(acc, i, j):
             for g in range(PASSES["x"]):
-                mx_pass(acc.rearrange("p k f -> p (k f)"), mx_operand[("x", i)], 256 * g + P * j,
-                        mx_operand[("w1", 0)], 256 * g, SUBNETS * SD, g == 0, False)
+                mx_pass(acc.rearrange("p k f -> p (k f)"), mx_operand[("x", i)], UNIT_ROWS * g + P * j,
+                        mx_operand[("w1", 0)], UNIT_ROWS * g, SUBNETS * SD, g == 0, False)
             for k in range(SUBNETS):
                 mx_pass(acc[:, k, :], mx_operand[("v", SUBNETS * i + k)], P * j,
-                        mx_operand[("w1", 0)], 256 * PASSES["x"] + SD * k, SD, False, k == SUBNETS - 1)
+                        mx_operand[("w1", 0)], UNIT_ROWS * PASSES["x"] + SD * k, SD, False, k == SUBNETS - 1)
 
         def finish(i):
-            for tiles in (((0,), (1,)) if i == STEPS - 1 else ((0, 1),)):
-                bank = psum.tile([P, len(tiles), SUBNETS, SD], F32, name="out_acc", tag="bank")
-                for n, j in enumerate(tiles):
-                    products(bank[:, n, :, :], i, j)
-                result = out_pool.tile([P, SUBNETS, len(tiles), SD], F32, name="result")
+            for row_tiles in (((0,), (1,)) if i == STEPS - 1 else ((0, 1),)):
+                bank = psum.tile([P, len(row_tiles), SUBNETS, SD], F32, name="out_acc", tag="bank")
+                for slot, j in enumerate(row_tiles):
+                    products(bank[:, slot, :, :], i, j)
+                result = out_pool.tile([P, SUBNETS, len(row_tiles), SD], F32, name="result")
                 nc.scalar.activation(out=result[:], in_=bank[:].rearrange("p j k f -> p k j f"), func=SILU)
-                nc.sync.dma_start(out=out_steps[i, :, :, SD * tiles[0]:SD * (tiles[0] + len(tiles))],
+                nc.sync.dma_start(out=out_steps[i, :, :, SD * row_tiles[0]:SD * (row_tiles[0] + len(row_tiles))],
                                   in_=result[:].rearrange("p k j f -> p k (j f)"))
 
         in_order_of_use = list(FIRST_UNITS)

from contextlib import ExitStack

import concourse.masks as masks
import concourse.mybir as mybir

F32 = mybir.dt.float32
BF16 = mybir.dt.bfloat16
U32 = mybir.dt.uint32
U8 = mybir.dt.uint8
FP8X4 = mybir.dt.float8_e4m3fn_x4
SILU = mybir.ActivationFunctionType.Silu

P = 128
ROWS, D, DV, SUBNETS, SD = 4096, 1024, 512, 2, 128
FLOPS = 2 * ROWS * SUBNETS * (D * DV + D * SD + DV * SD)

K_PASS = 4 * P
WORDS = K_PASS // 2
UNIT_ROWS = 2 * P

STEPS = ROWS // UNIT_ROWS
LAG = 2
RAW_BUFS = 8

PASSES = {"x": D // K_PASS, "h": D // K_PASS, "wv": D // K_PASS, "w1": (D + DV) // K_PASS}
WEIGHTS = ("wv", "w1")
FIRST_UNITS = (("h", 0), ("wv", 0), ("wv", 1), ("wv", 2), ("wv", 3), ("h", 1))


def units_before_step(i):
    units = [("h", n) for n in (i + 1, i + 2) if n < STEPS]
    units.append(("x", i - 1))
    if i == 1:
        units.append(("w1", 0))
    units.append(("x", i))
    return units


def tile_distributedb_pa_t_kernel(tc, x, h, Wv, W1, out):
    nc = tc.nc
    sources = {
        "x": x.rearrange("b (i p j) d -> (b i) p j d", p=P, j=2),
        "h": h.rearrange("b (i p j) d -> (b i) p j d", p=P, j=2),
        "wv": Wv.rearrange("k (u p e) d -> (k u) p e d", u=2, p=P, e=2),
        "w1": W1.rearrange("(o k) p d -> o p k d", o=1),
    }
    out_steps = out.rearrange("k b (i p j) f -> (b i) p k (j f)", p=P, j=2)

    with ExitStack() as ctx:
        keep = ctx.enter_context(tc.tile_pool(name="keep", bufs=1))
        raw_pool = ctx.enter_context(tc.tile_pool(name="raw", bufs=RAW_BUFS))
        bf16_pool = ctx.enter_context(tc.tile_pool(name="bf16", bufs=4))
        mx_pool = ctx.enter_context(tc.tile_pool(name="mx", bufs=6))
        out_pool = ctx.enter_context(tc.tile_pool(name="outs", bufs=5))
        psum = ctx.enter_context(tc.psum_pool(name="psum", bufs=8))
        ctx.enter_context(tc.manual_schedule())

        identity = keep.tile([P, P], F32, name="identity")
        masks.make_identity(nc, identity[:])
        dummy = keep.tile([P, 8], F32, name="dummy")
        nc.vector.memset(dummy[:], 0.0)
        nc.scalar.activation(out=dummy[:], in_=dummy[:], func=SILU)

        raw = {}
        mx_operand = {}
        regrouped = {}

        def new_tile(pool, unit, role, width, dtype):
            kind, n = unit
            if kind in WEIGHTS:
                return keep.tile([P, width], dtype, name="%s%d_%s" % (kind, n, role), align_bytes=64)
            return pool.tile([P, width], dtype, name=kind + "_" + role, tag=kind + "_" + role, align_bytes=64)

        def load(unit):
            kind, n = unit
            raw[unit] = new_tile(raw_pool, unit, "raw", 2 * K_PASS * PASSES[kind], BF16)
            nc.sync.dma_start(out=raw[unit][:].rearrange("p (s d) -> p s d", s=2), in_=sources[kind][n, :, :, :])

        def quantise(values, unit):
            width = values.shape[1]
            codes = new_tile(mx_pool, unit, "codes", width // 4, U32)
            scales = new_tile(mx_pool, unit, "scales", width // 4, U8)
            for col in range(0, width, 2048):
                end = min(col + 2048, width)
                nc.vector.quantize_mx(
                    out=codes[:, col // 4:end // 4].bitcast(FP8X4),
                    scales=scales[:, col // 4:end // 4],
                    in_=values[:, col:end],
                )
            mx_operand[unit] = (codes, scales)

        def quantise_views(before):
            for half in sorted(regrouped):
                if half < before and ("v", half) not in mx_operand:
                    quantise(regrouped[half][:], ("v", half))

        def transpose_run(units):
            quantise_views(before=len(regrouped))
            copies = (nc.vector.tensor_copy, nc.scalar.copy)
            grouped = {}
            banks = 0
            for unit in units:
                passes = PASSES[unit[0]]
                words = raw[unit][:].bitcast(F32)
                grouped[unit] = new_tile(bf16_pool, unit, "grouped", 2 * K_PASS * passes, BF16)
                dest = grouped[unit][:].bitcast(F32).rearrange("p (g r u) -> p g r u", r=UNIT_ROWS, u=2)
                for g in range(passes):
                    bank = psum.tile([P, 2, UNIT_ROWS], F32, name="flipped", tag="bank")
                    for u in range(2):
                        for s in range(2):
                            first = WORDS * (passes * s + g) + P * u
                            nc.tensor.transpose(bank[:, u, P * s:P * (s + 1)], words[:, first:first + P], identity[:])
                    copies[banks % 2](out=dest[:, g], in_=bank[:].rearrange("p u r -> p r u"))
                    banks += 1
            for kind, n in units:
                if kind not in WEIGHTS and n + RAW_BUFS < STEPS:
                    load((kind, n + RAW_BUFS))
            for unit in units:
                quantise(grouped[unit][:], unit)

        def mx_pass(acc, stationary, s_col, moving, m_col, m_cols, start, stop):
            nc.tensor.matmul_mx(
                out=acc,
                lhsT=stationary[0][:, s_col:s_col + P].bitcast(FP8X4),
                lhsT_scale=stationary[1][:, s_col:s_col + P],
                rhs=moving[0][:, m_col:m_col + m_cols].bitcast(FP8X4),
                rhs_scale=moving[1][:, m_col:m_col + m_cols],
                start=start,
                stop=stop,
            )

        def views(i):
            for k in range(SUBNETS):
                half = SUBNETS * i + k
                by_tile = bf16_pool.tile([P, 4, UNIT_ROWS], BF16, name="views_by_tile")
                for u in range(2):
                    bank = psum.tile([P, 2, UNIT_ROWS], F32, name="views_acc", tag="bank")
                    for e in range(2):
                        for g in range(PASSES["h"]):
                            mx_pass(bank[:, e, :], mx_operand[("wv", 2 * k + u)], UNIT_ROWS * g + P * e,
                                    mx_operand[("h", i)], UNIT_ROWS * g, UNIT_ROWS, g == 0, g == PASSES["h"] - 1)
                    nc.scalar.copy(out=by_tile[:, 2 * u:2 * u + 2, :], in_=bank[:])
                regrouped[half] = bf16_pool.tile([P, 4 * UNIT_ROWS], BF16, name="views_regrouped", align_bytes=64)
                nc.vector.tensor_copy(
                    out=regrouped[half][:].rearrange("p (a r t) -> p a t r", r=4, t=4),
                    in_=by_tile[:].rearrange("p t (a r) -> p a t r", r=4),
                )
                quantise_views(before=half + 1 if i == STEPS - 1 else half)

        def products(acc, i, j):
            for g in range(PASSES["x"]):
                mx_pass(acc.rearrange("p k f -> p (k f)"), mx_operand[("x", i)], UNIT_ROWS * g + P * j,
                        mx_operand[("w1", 0)], UNIT_ROWS * g, SUBNETS * SD, g == 0, False)
            for k in range(SUBNETS):
                mx_pass(acc[:, k, :], mx_operand[("v", SUBNETS * i + k)], P * j,
                        mx_operand[("w1", 0)], UNIT_ROWS * PASSES["x"] + SD * k, SD, False, k == SUBNETS - 1)

        def finish(i):
            for row_tiles in (((0,), (1,)) if i == STEPS - 1 else ((0, 1),)):
                bank = psum.tile([P, len(row_tiles), SUBNETS, SD], F32, name="out_acc", tag="bank")
                for slot, j in enumerate(row_tiles):
                    products(bank[:, slot, :, :], i, j)
                result = out_pool.tile([P, SUBNETS, len(row_tiles), SD], F32, name="result")
                nc.scalar.activation(out=result[:], in_=bank[:].rearrange("p j k f -> p k j f"), func=SILU)
                nc.sync.dma_start(out=out_steps[i, :, :, SD * row_tiles[0]:SD * (row_tiles[0] + len(row_tiles))],
                                  in_=result[:].rearrange("p k j f -> p k (j f)"))

        in_order_of_use = list(FIRST_UNITS)
        for i in range(1, STEPS, 2):
            in_order_of_use.extend(units_before_step(i))
        for unit in in_order_of_use:
            if unit[0] in WEIGHTS or unit[1] < RAW_BUFS:
                load(unit)

        for unit in FIRST_UNITS:
            transpose_run([unit])
        for i in range(STEPS + LAG):
            if i % 2 == 1 and i < STEPS:
                transpose_run(units_before_step(i))
            if i < STEPS:
                views(i)
            if i >= LAG:
                finish(i - LAG)
